import numpy as np
import ml_dtypes


def mxq(x, axis, fmt="e4m3"):
    dtype, down = {"e4m3": (ml_dtypes.float8_e4m3fn, 7), "e5m2": (ml_dtypes.float8_e5m2, 14)}[fmt]
    v = np.moveaxis(np.asarray(x, np.float32).astype(ml_dtypes.bfloat16).astype(np.float64), axis, -1)
    blocks = v.reshape(v.shape[:-1] + (-1, 32))
    amax = np.abs(blocks).max(-1, keepdims=True)
    byte = np.maximum(np.where(amax > 0, np.frexp(amax)[1] - 1 + 127, 0) - down, 1)
    scale = np.exp2(byte - 127.0)
    codes = (blocks / scale).astype(np.float32).astype(dtype).astype(np.float64)
    return np.moveaxis((codes * scale).reshape(v.shape), -1, axis)


WIDE = False


def mx_kscale(k):
    if not WIDE:
        return np.ones(k)
    levels = np.array([20, -20, 10, -10, 0])
    a = np.random.permutation(np.resize(levels, k // 512 * 4)).reshape(k // 512, 4)
    idx = np.arange(k)
    return np.exp2(a[idx // 512, idx % 128 // 32])


BF16 = ml_dtypes.bfloat16


def bf(x):
    return np.asarray(x, np.float32).astype(BF16)


def f64(x):
    return np.asarray(x).astype(np.float64)


B, H, T, S, D = 2, 4, 1024, 512, 512


def setup_inputs():
    u = mx_kscale(D)
    aw = np.random.uniform(0.0, 1.0, (B, H, T, S))
    aw = aw / aw.sum(-1, keepdims=True)
    v = np.random.standard_normal((B, H, S, D)) * 8.0 / u
    g = np.random.standard_normal((B, T, H * D)) * np.exp2(np.random.randint(-12, 1, (B, T, 1))) * 0.5 * np.tile(u, H)
    return {"attn_weights": bf(aw), "v": bf(v), "batch_size": B, "tgt_len": T, "grad_out": bf(g)}


def reference(attn_weights, v, batch_size, tgt_len, grad_out):
    vv = f64(v)
    h, d = vv.shape[1], vv.shape[3]
    g = f64(grad_out).reshape(batch_size, tgt_len, h, d).transpose(0, 2, 1, 3)
    return mxq(g, 3, "e5m2") @ mxq(vv, 3, "e4m3").transpose(0, 1, 3, 2)

@@ -1,0 +1,178 @@
+from contextlib import ExitStack
+
+import concourse.mybir as mybir
+from concourse.masks import make_identity
+
+BF16 = mybir.dt.bfloat16
+F32 = mybir.dt.float32
+U32 = mybir.dt.uint32
+U8 = mybir.dt.uint8
+E4 = mybir.dt.float8_e4m3fn_x4
+E5 = mybir.dt.float8_e5m2_x4
+
+P = 128
+B, H, T, S, D = 2, 4, 1024, 512, 512
+J = T // P
+FLOPS = 2 * B * H * T * S * D
+BYTES = 2 * (B * T * H * D + B * H * S * D) + 4 * B * H * T * S
+
+PIN = False
+BIG_BUFS = 10
+
+
+def tile_attentionweightedvalues_kernel(
+    tc, attn_weights, v, batch_size, tgt_len, grad_out, out
+):
+    nc = tc.nc
+    g_view = grad_out.rearrange("b (p j) c -> b p (j c)", j=J)
+    v_view = v.rearrange("b h (p i) d -> b p h (i d)", i=4)
+    o_view = out.rearrange("b h (p j) s -> b h p (j s)", j=J)
+
+    with ExitStack() as ctx:
+        const = ctx.enter_context(tc.tile_pool(name="const", bufs=1))
+        big = ctx.enter_context(tc.tile_pool(name="big", bufs=BIG_BUFS))
+        grp = ctx.enter_context(tc.tile_pool(name="grp", bufs=2))
+        gcp = ctx.enter_context(tc.tile_pool(name="gcp", bufs=3))
+        vcp = ctx.enter_context(tc.tile_pool(name="vcp", bufs=1))
+        tp = ctx.enter_context(tc.psum_pool(name="tp", bufs=4))
+        accp = ctx.enter_context(tc.psum_pool(name="accp", bufs=4))
+        if PIN:
+            ctx.enter_context(tc.manual_schedule())
+
+        ident = const.tile([P, P], F32, name="ident")
+        make_identity(nc, ident[:])
+
+        v_raw = []
+        g_raw = []
+        for b in range(B):
+            vr = big.tile([P, H, 4 * D], BF16, tag="big", name="v_raw%d" % b)
+            v_raw.append(vr)
+            if b == 0:
+                nc.sync.dma_start(out=vr[:, 0:2, :], in_=v_view[b, :, 0:2, :])
+                nc.sync.dma_start(out=vr[:, 2:4, :], in_=v_view[b, :, 2:4, :])
+            else:
+                nc.sync.dma_start(out=vr[:], in_=v_view[b])
+            quads = []
+            for q in range(2):
+                gr = big.tile([P, 4 * H * D], BF16, tag="big", name="g_raw%d_%d" % (b, q))
+                quads.append(gr)
+                w = 4 * H * D
+                if b == 0 and q == 0:
+                    hw = w // 2
+                    nc.sync.dma_start(out=gr[:, 0:hw], in_=g_view[b, :, 0:hw])
+                    nc.sync.dma_start(out=gr[:, hw:w], in_=g_view[b, :, hw:w])
+                else:
+                    nc.sync.dma_start(out=gr[:], in_=g_view[b, :, q * w : (q + 1) * w])
+            g_raw.append(quads)
+
+        items = [
+            ("V", 0, 0), ("V", 0, 1), ("V", 0, 2), ("V", 0, 3),
+            ("G", 0, 0), ("G", 0, 1), ("V", 1, 0), ("G", 0, 2), ("V", 1, 1),
+            ("G", 0, 3), ("V", 1, 2), ("V", 1, 3),
+            ("G", 1, 0), ("G", 1, 1), ("G", 1, 2), ("G", 1, 3),
+        ]
+        on_scalar = {("V", 0, 1): (0, 1), ("V", 0, 3): (0, 1), ("G", 0, 0): (2, 3)}
+
+        banks = {}
+        grouped = {}
+        codes = {}
+        outs = {}
+
+        def transposes(item):
+            kind, b, x = item
+            if kind == "V":
+                src = v_raw[b][:].rearrange("p h e -> p (h e)").bitcast(F32)
+                base = x * 1024
+                nb = 2
+            else:
+                src = g_raw[b][x // 2][:].bitcast(F32)
+                base = (x % 2) * 2048
+                nb = 4
+            lst = []
+            for n in range(nb):
+                bank = tp.tile([P, 4, P], F32, tag="tp", name="tpb")
+                for s in range(4):
+                    o = base + (4 * n + s) * P
+                    nc.tensor.transpose(out=bank[:, s, :], in_=src[:, o : o + P], identity=ident[:])
+                lst.append(bank)
+            banks[item] = lst
+
+        def copy_out(item, n):
+            kind = item[0]
+            if item not in grouped:
+                if kind == "V":
+                    grouped[item] = grp.tile([P, 4 * S], BF16, tag="gv", name="gv", align_bytes=64)
+                else:
+                    grouped[item] = grp.tile([P, 4 * 8 * P], BF16, tag="gg", name="gg", align_bytes=64)
+            gf = grouped[item][:].bitcast(F32)
+            bank = banks[item][n]
+            if kind == "V":
+                dst = gf.rearrange("p (r a x) -> p a r x", a=2, x=4)[:, n]
+                src = bank[:].rearrange("p x r -> p r x")
+            else:
+                dst = gf[:, n * 512 : (n + 1) * 512].rearrange("p (x r u) -> p x r u", x=2, u=2)
+                src = bank[:].rearrange("p (x u) r -> p x r u", u=2)
+            if n in on_scalar.get(item, ()):
+                nc.scalar.copy(out=dst, in_=src)
+            else:
+                nc.vector.tensor_copy(out=dst, in_=src)
+
+        def quantise(item):
+            kind, b, x = item
+            if kind == "V":
+                c = vcp.tile([P, S], U32, name="vc%d_%d" % (b, x), align_bytes=64)
+                s = vcp.tile([P, S], U8, name="vs%d_%d" % (b, x), align_bytes=64)
+                nc.vector.quantize_mx(out=c[:].bitcast(E4), scales=s[:], in_=grouped[item][:])
+            else:
+                c = gcp.tile([P, 8 * P], U32, tag="gc", name="gc", align_bytes=64)
+                s = gcp.tile([P, 8 * P], U8, tag="gs", name="gs", align_bytes=64)
+                nc.vector.quantize_mx(out=c[:].bitcast(E5), scales=s[:], in_=grouped[item][:])
+            codes[item] = (c, s)
+
+        def passes(item, heads):
+            kind, b, x = item
+            if kind == "V":
+                return
+            gc, gs = codes[item]
+            for h in heads:
+                vc, vs = codes[("V", b, h)]
+                for jl in range(2):
+                    j = 2 * x + jl
+                    u0 = (jl * 4 + h) * P
+                    acc = accp.tile([P, S], F32, tag="acc", name="acc")
+                    nc.tensor.matmul_mx(
+                        out=acc[:],
+                        lhsT=gc[:, u0 : u0 + P].bitcast(E5),
+                        lhsT_scale=gs[:, u0 : u0 + P],
+                        rhs=vc[:].bitcast(E4),
+                        rhs_scale=vs[:],
+                        start=True,
+                        stop=True,
+                    )
+                    key = (b, h // 2, j // 4)
+                    if key not in outs:
+                        outs[key] = big.tile([P, 2, 4 * S], F32, tag="big", name="ot%d_%d_%d" % key)
+                    ot = outs[key]
+                    jq = j % 4
+                    nc.scalar.copy(out=ot[:, h % 2, jq * S : (jq + 1) * S], in_=acc[:])
+                    if jq == 3:
+                        q = j // 4
+                        nc.sync.dma_start(
+                            out=o_view[b, h, :, q * 4 * S : (q + 1) * 4 * S], in_=ot[:, h % 2, :]
+                        )
+
+        n_items = len(items)
+        transposes(items[0])
+        for k in range(n_items + 1):
+            if k < n_items:
+                copy_out(items[k], 0)
+            if k >= 1:
+                quantise(items[k - 1])
+                passes(items[k - 1], (0, 1))
+            if k + 1 < n_items:
+                transposes(items[k + 1])
+            if k < n_items:
+                for n in range(1, len(banks[items[k]])):
+                    copy_out(items[k], n)
+            if k >= 1:
+                passes(items[k - 1], (2, 3))

@@ -13,11 +13,13 @@ E5 = mybir.dt.float8_e5m2_x4
 P = 128
 B, H, T, S, D = 2, 4, 1024, 512, 512
 J = T // P
+R = 4
 FLOPS = 2 * B * H * T * S * D
 BYTES = 2 * (B * T * H * D + B * H * S * D) + 4 * B * H * T * S
 
-PIN = False
-BIG_BUFS = 10
+PIN = True
+BIG_BUFS = 9
+LAG_M = 3
 
 
 def tile_attentionweightedvalues_kernel(
@@ -31,9 +33,8 @@ def tile_attentionweightedvalues_kernel(
     with ExitStack() as ctx:
         const = ctx.enter_context(tc.tile_pool(name="const", bufs=1))
         big = ctx.enter_context(tc.tile_pool(name="big", bufs=BIG_BUFS))
-        grp = ctx.enter_context(tc.tile_pool(name="grp", bufs=2))
-        gcp = ctx.enter_context(tc.tile_pool(name="gcp", bufs=3))
-        vcp = ctx.enter_context(tc.tile_pool(name="vcp", bufs=1))
+        grp = ctx.enter_context(tc.tile_pool(name="grp", bufs=3))
+        cod = ctx.enter_context(tc.tile_pool(name="cod", bufs=1))
         tp = ctx.enter_context(tc.psum_pool(name="tp", bufs=4))
         accp = ctx.enter_context(tc.psum_pool(name="accp", bufs=4))
         if PIN:
@@ -42,137 +43,127 @@ def tile_attentionweightedvalues_kernel(
         ident = const.tile([P, P], F32, name="ident")
         make_identity(nc, ident[:])
 
-        v_raw = []
-        g_raw = []
-        for b in range(B):
-            vr = big.tile([P, H, 4 * D], BF16, tag="big", name="v_raw%d" % b)
-            v_raw.append(vr)
-            if b == 0:
-                nc.sync.dma_start(out=vr[:, 0:2, :], in_=v_view[b, :, 0:2, :])
-                nc.sync.dma_start(out=vr[:, 2:4, :], in_=v_view[b, :, 2:4, :])
-            else:
-                nc.sync.dma_start(out=vr[:], in_=v_view[b])
-            quads = []
-            for q in range(2):
-                gr = big.tile([P, 4 * H * D], BF16, tag="big", name="g_raw%d_%d" % (b, q))
-                quads.append(gr)
-                w = 4 * H * D
-                if b == 0 and q == 0:
-                    hw = w // 2
-                    nc.sync.dma_start(out=gr[:, 0:hw], in_=g_view[b, :, 0:hw])
-                    nc.sync.dma_start(out=gr[:, hw:w], in_=g_view[b, :, hw:w])
-                else:
-                    nc.sync.dma_start(out=gr[:], in_=g_view[b, :, q * w : (q + 1) * w])
-            g_raw.append(quads)
-
-        items = [
-            ("V", 0, 0), ("V", 0, 1), ("V", 0, 2), ("V", 0, 3),
-            ("G", 0, 0), ("G", 0, 1), ("V", 1, 0), ("G", 0, 2), ("V", 1, 1),
-            ("G", 0, 3), ("V", 1, 2), ("V", 1, 3),
-            ("G", 1, 0), ("G", 1, 1), ("G", 1, 2), ("G", 1, 3),
+        v_raw = [big.tile([P, H, 4 * D], BF16, tag="big", name="v_raw%d" % b) for b in range(B)]
+        g_raw = [
+            [big.tile([P, 4 * H * D], BF16, tag="big", name="g_raw%d_%d" % (b, q)) for q in range(2)]
+            for b in range(B)
         ]
-        on_scalar = {("V", 0, 1): (0, 1), ("V", 0, 3): (0, 1), ("G", 0, 0): (2, 3)}
+        w = 4 * H * D
+        for h in range(H):
+            nc.sync.dma_start(out=v_raw[0][:, h, :], in_=v_view[0, :, h, :])
+        nc.sync.dma_start(out=g_raw[0][0][:, 0 : w // 2], in_=g_view[0, :, 0 : w // 2])
+        nc.sync.dma_start(out=g_raw[0][0][:, w // 2 : w], in_=g_view[0, :, w // 2 : w])
+        nc.sync.dma_start(out=g_raw[0][1][:], in_=g_view[0, :, w : 2 * w])
+        nc.sync.dma_start(out=v_raw[1][:], in_=v_view[1])
+        nc.sync.dma_start(out=g_raw[1][0][:], in_=g_view[1, :, 0:w])
+        nc.sync.dma_start(out=g_raw[1][1][:], in_=g_view[1, :, w : 2 * w])
+
+        units = [("V", 0, h) for h in range(H)]
+        units += [("G", 0, j) for j in range(6)]
+        units += [("V", 1, 0), ("G", 0, 6), ("V", 1, 1), ("G", 0, 7), ("V", 1, 2), ("V", 1, 3)]
+        units += [("G", 1, j) for j in range(J)]
 
         banks = {}
         grouped = {}
         codes = {}
+        accs = {}
         outs = {}
 
-        def transposes(item):
-            kind, b, x = item
+        def transposes(unit):
+            kind, b, x = unit
             if kind == "V":
-                src = v_raw[b][:].rearrange("p h e -> p (h e)").bitcast(F32)
-                base = x * 1024
-                nb = 2
+                src = v_raw[b][:, x, :].bitcast(F32)
             else:
-                src = g_raw[b][x // 2][:].bitcast(F32)
-                base = (x % 2) * 2048
-                nb = 4
+                src = g_raw[b][x // 4][:, (x % 4) * 2048 : (x % 4 + 1) * 2048].bitcast(F32)
             lst = []
-            for n in range(nb):
+            for n in range(2):
                 bank = tp.tile([P, 4, P], F32, tag="tp", name="tpb")
                 for s in range(4):
-                    o = base + (4 * n + s) * P
+                    o = (4 * n + s) * P
                     nc.tensor.transpose(out=bank[:, s, :], in_=src[:, o : o + P], identity=ident[:])
                 lst.append(bank)
-            banks[item] = lst
+            banks[unit] = lst
 
-        def copy_out(item, n):
-            kind = item[0]
-            if item not in grouped:
-                if kind == "V":
-                    grouped[item] = grp.tile([P, 4 * S], BF16, tag="gv", name="gv", align_bytes=64)
-                else:
-                    grouped[item] = grp.tile([P, 4 * 8 * P], BF16, tag="gg", name="gg", align_bytes=64)
-            gf = grouped[item][:].bitcast(F32)
-            bank = banks[item][n]
+        def copy_out(unit, n):
+            kind = unit[0]
+            if unit not in grouped:
+                grouped[unit] = grp.tile([P, 2048], BF16, tag="grp", name="grp", align_bytes=64)
+            gf = grouped[unit][:].bitcast(F32)
+            bank = banks[unit][n]
             if kind == "V":
                 dst = gf.rearrange("p (r a x) -> p a r x", a=2, x=4)[:, n]
                 src = bank[:].rearrange("p x r -> p r x")
+                nc.scalar.copy(out=dst, in_=src)
             else:
                 dst = gf[:, n * 512 : (n + 1) * 512].rearrange("p (x r u) -> p x r u", x=2, u=2)
                 src = bank[:].rearrange("p (x u) r -> p x r u", u=2)
-            if n in on_scalar.get(item, ()):
-                nc.scalar.copy(out=dst, in_=src)
+                if n == 0:
+                    nc.vector.tensor_copy(out=dst, in_=src)
+                else:
+                    nc.scalar.copy(out=dst, in_=src)
+
+        def quantise(unit):
+            c = cod.tile([P, 512], U32, name="c%s%d_%d" % unit, align_bytes=64)
+            s = cod.tile([P, 512], U8, name="s%s%d_%d" % unit, align_bytes=64)
+            fmt = E4 if unit[0] == "V" else E5
+            nc.vector.quantize_mx(out=c[:].bitcast(fmt), scales=s[:], in_=grouped[unit][:])
+            codes[unit] = (c, s)
+
+        def multiply(b, h, j):
+            gc, gs = codes[("G", b, j)]
+            vc, vs = codes[("V", b, h)]
+            acc = accp.tile([P, S], F32, tag="acc", name="acc")
+            nc.tensor.matmul_mx(
+                out=acc[:],
+                lhsT=gc[:, h * P : (h + 1) * P].bitcast(E5),
+                lhsT_scale=gs[:, h * P : (h + 1) * P],
+                rhs=vc[:].bitcast(E4),
+                rhs_scale=vs[:],
+                start=True,
+                stop=True,
+            )
+            accs[(b, h, j)] = acc
+
+        def empty(b, h, j, on_vector):
+            key = (b, h // 2, j // R)
+            if key not in outs:
+                outs[key] = big.tile([P, 2, R * S], F32, tag="big", name="ot%d_%d_%d" % key)
+            ot = outs[key]
+            jr = j % R
+            dst = ot[:, h % 2, jr * S : (jr + 1) * S]
+            if on_vector:
+                nc.vector.tensor_copy(out=dst, in_=accs[(b, h, j)][:])
             else:
-                nc.vector.tensor_copy(out=dst, in_=src)
+                nc.scalar.copy(out=dst, in_=accs[(b, h, j)][:])
+            if jr == R - 1:
+                q = j // R
+                nc.sync.dma_start(
+                    out=o_view[b, h, :, q * R * S : (q + 1) * R * S], in_=ot[:, h % 2, :]
+                )
 
-        def quantise(item):
-            kind, b, x = item
-            if kind == "V":
-                c = vcp.tile([P, S], U32, name="vc%d_%d" % (b, x), align_bytes=64)
-                s = vcp.tile([P, S], U8, name="vs%d_%d" % (b, x), align_bytes=64)
-                nc.vector.quantize_mx(out=c[:].bitcast(E4), scales=s[:], in_=grouped[item][:])
-            else:
-                c = gcp.tile([P, 8 * P], U32, tag="gc", name="gc", align_bytes=64)
-                s = gcp.tile([P, 8 * P], U8, tag="gs", name="gs", align_bytes=64)
-                nc.vector.quantize_mx(out=c[:].bitcast(E5), scales=s[:], in_=grouped[item][:])
-            codes[item] = (c, s)
-
-        def passes(item, heads):
-            kind, b, x = item
-            if kind == "V":
-                return
-            gc, gs = codes[item]
-            for h in heads:
-                vc, vs = codes[("V", b, h)]
-                for jl in range(2):
-                    j = 2 * x + jl
-                    u0 = (jl * 4 + h) * P
-                    acc = accp.tile([P, S], F32, tag="acc", name="acc")
-                    nc.tensor.matmul_mx(
-                        out=acc[:],
-                        lhsT=gc[:, u0 : u0 + P].bitcast(E5),
-                        lhsT_scale=gs[:, u0 : u0 + P],
-                        rhs=vc[:].bitcast(E4),
-                        rhs_scale=vs[:],
-                        start=True,
-                        stop=True,
-                    )
-                    key = (b, h // 2, j // 4)
-                    if key not in outs:
-                        outs[key] = big.tile([P, 2, 4 * S], F32, tag="big", name="ot%d_%d_%d" % key)
-                    ot = outs[key]
-                    jq = j % 4
-                    nc.scalar.copy(out=ot[:, h % 2, jq * S : (jq + 1) * S], in_=acc[:])
-                    if jq == 3:
-                        q = j // 4
-                        nc.sync.dma_start(
-                            out=o_view[b, h, :, q * 4 * S : (q + 1) * 4 * S], in_=ot[:, h % 2, :]
-                        )
-
-        n_items = len(items)
-        transposes(items[0])
-        for k in range(n_items + 1):
-            if k < n_items:
-                copy_out(items[k], 0)
-            if k >= 1:
-                quantise(items[k - 1])
-                passes(items[k - 1], (0, 1))
-            if k + 1 < n_items:
-                transposes(items[k + 1])
-            if k < n_items:
-                for n in range(1, len(banks[items[k]])):
-                    copy_out(items[k], n)
-            if k >= 1:
-                passes(items[k - 1], (2, 3))
+        n_units = len(units)
+        n_g = 0
+        for s in range(n_units + LAG_M + 1):
+            a = units[s - 1] if 1 <= s <= n_units else None
+            q = units[s - 2] if 2 <= s <= n_units + 1 else None
+            m = units[s - LAG_M] if LAG_M <= s < n_units + LAG_M else None
+            share = 0
+            if m is not None and m[0] == "G":
+                share = 1 + n_g % 2
+                n_g += 1
+                for h in range(H):
+                    multiply(m[1], h, m[2])
+            if s < n_units:
+                transposes(units[s])
+            if q is not None:
+                quantise(q)
+            if a is not None:
+                copy_out(a, 0)
+            if m is not None and m[0] == "G":
+                for h in range(share):
+                    empty(m[1], h, m[2], True)
+            if a is not None:
+                copy_out(a, 1)
+            if m is not None and m[0] == "G":
+                for h in range(share, H):
+                    empty(m[1], h, m[2], False)

@@ -13,13 +13,16 @@ E5 = mybir.dt.float8_e5m2_x4
 P = 128
 B, H, T, S, D = 2, 4, 1024, 512, 512
 J = T // P
-R = 4
+R = 8
 FLOPS = 2 * B * H * T * S * D
 BYTES = 2 * (B * T * H * D + B * H * S * D) + 4 * B * H * T * S
 
 PIN = True
 BIG_BUFS = 9
 LAG_M = 3
+QUOTA = 3
+T_COPY = 440
+T_QUANT = 465
 
 
 def tile_attentionweightedvalues_kernel(
@@ -49,19 +52,29 @@ def tile_attentionweightedvalues_kernel(
             for b in range(B)
         ]
         w = 4 * H * D
-        for h in range(H):
-            nc.sync.dma_start(out=v_raw[0][:, h, :], in_=v_view[0, :, h, :])
+        nc.sync.dma_start(out=v_raw[0][:, 0, :], in_=v_view[0, :, 0, :])
+        nc.sync.dma_start(out=v_raw[0][:, 1, :], in_=v_view[0, :, 1, :])
         nc.sync.dma_start(out=g_raw[0][0][:, 0 : w // 2], in_=g_view[0, :, 0 : w // 2])
         nc.sync.dma_start(out=g_raw[0][0][:, w // 2 : w], in_=g_view[0, :, w // 2 : w])
         nc.sync.dma_start(out=g_raw[0][1][:], in_=g_view[0, :, w : 2 * w])
-        nc.sync.dma_start(out=v_raw[1][:], in_=v_view[1])
+        nc.sync.dma_start(out=v_raw[0][:, 2:4, :], in_=v_view[0, :, 2:4, :])
+        nc.sync.dma_start(out=v_raw[1][:, 0, :], in_=v_view[1, :, 0, :])
         nc.sync.dma_start(out=g_raw[1][0][:], in_=g_view[1, :, 0:w])
         nc.sync.dma_start(out=g_raw[1][1][:], in_=g_view[1, :, w : 2 * w])
+        nc.sync.dma_start(out=v_raw[1][:, 1:4, :], in_=v_view[1, :, 1:4, :])
 
-        units = [("V", 0, h) for h in range(H)]
-        units += [("G", 0, j) for j in range(6)]
-        units += [("V", 1, 0), ("G", 0, 6), ("V", 1, 1), ("G", 0, 7), ("V", 1, 2), ("V", 1, 3)]
-        units += [("G", 1, j) for j in range(J)]
+        units = [("V", 0, 0), ("V", 0, 1)] + [("G", 0, j) for j in range(J)]
+        units += [("V", 0, 2), ("V", 0, 3), ("V", 1, 0)] + [("G", 1, j) for j in range(J)]
+        units += [("V", 1, 1), ("V", 1, 2), ("V", 1, 3)]
+        place = {}
+        for k, unit in enumerate(units):
+            place[unit] = k
+
+        todo = []
+        for j in range(J):
+            todo += [(0, 0, j), (0, 1, j)]
+        for b, h in ((0, 2), (0, 3), (1, 0), (1, 1), (1, 2), (1, 3)):
+            todo += [(b, h, j) for j in range(J)]
 
         banks = {}
         grouped = {}
@@ -125,45 +138,60 @@ def tile_attentionweightedvalues_kernel(
             accs[(b, h, j)] = acc
 
         def empty(b, h, j, on_vector):
-            key = (b, h // 2, j // R)
+            key = (b, h)
             if key not in outs:
-                outs[key] = big.tile([P, 2, R * S], F32, tag="big", name="ot%d_%d_%d" % key)
+                outs[key] = big.tile([P, J * S], F32, tag="big", name="ot%d_%d" % key)
             ot = outs[key]
-            jr = j % R
-            dst = ot[:, h % 2, jr * S : (jr + 1) * S]
+            dst = ot[:, j * S : (j + 1) * S]
             if on_vector:
                 nc.vector.tensor_copy(out=dst, in_=accs[(b, h, j)][:])
             else:
                 nc.scalar.copy(out=dst, in_=accs[(b, h, j)][:])
-            if jr == R - 1:
-                q = j // R
-                nc.sync.dma_start(
-                    out=o_view[b, h, :, q * R * S : (q + 1) * R * S], in_=ot[:, h % 2, :]
-                )
+            if j == J - 1:
+                nc.sync.dma_start(out=o_view[b, h], in_=ot[:])
 
         n_units = len(units)
-        n_g = 0
-        for s in range(n_units + LAG_M + 1):
+        work_v = 0
+        work_s = 0
+        done = 0
+        s = 0
+        while s < n_units + 2 or done < len(todo):
             a = units[s - 1] if 1 <= s <= n_units else None
             q = units[s - 2] if 2 <= s <= n_units + 1 else None
-            m = units[s - LAG_M] if LAG_M <= s < n_units + LAG_M else None
-            share = 0
-            if m is not None and m[0] == "G":
-                share = 1 + n_g % 2
-                n_g += 1
-                for h in range(H):
-                    multiply(m[1], h, m[2])
+            run = []
+            while len(run) < QUOTA and done < len(todo):
+                b, h, j = todo[done]
+                if max(place[("G", b, j)], place[("V", b, h)]) > s - LAG_M:
+                    break
+                run.append(todo[done])
+                done += 1
+            for b, h, j in run:
+                multiply(b, h, j)
             if s < n_units:
                 transposes(units[s])
+            if q is not None:
+                work_v += T_QUANT
+            if a is not None:
+                if a[0] == "V":
+                    work_s += 2 * T_COPY
+                else:
+                    work_v += T_COPY
+                    work_s += T_COPY
+            share = 0
+            for k in range(len(run)):
+                if work_v <= work_s:
+                    work_v += T_COPY
+                    share += 1
+                else:
+                    work_s += T_COPY
             if q is not None:
                 quantise(q)
             if a is not None:
                 copy_out(a, 0)
-            if m is not None and m[0] == "G":
-                for h in range(share):
-                    empty(m[1], h, m[2], True)
+            for b, h, j in run[:share]:
+                empty(b, h, j, True)
             if a is not None:
                 copy_out(a, 1)
-            if m is not None and m[0] == "G":
-                for h in range(share, H):
-                    empty(m[1], h, m[2], False)
+            for b, h, j in run[share:]:
+                empty(b, h, j, False)
+            s += 1

@@ -17,7 +17,7 @@ R = 8
 FLOPS = 2 * B * H * T * S * D
 BYTES = 2 * (B * T * H * D + B * H * S * D) + 4 * B * H * T * S
 
-PIN = True
+PIN = False
 BIG_BUFS = 9
 LAG_M = 3
 QUOTA = 3

@@ -7,22 +7,22 @@ BF16 = mybir.dt.bfloat16
 F32 = mybir.dt.float32
 U32 = mybir.dt.uint32
 U8 = mybir.dt.uint8
-E4 = mybir.dt.float8_e4m3fn_x4
-E5 = mybir.dt.float8_e5m2_x4
+E4M3_X4 = mybir.dt.float8_e4m3fn_x4
+E5M2_X4 = mybir.dt.float8_e5m2_x4
 
 P = 128
 B, H, T, S, D = 2, 4, 1024, 512, 512
 J = T // P
-R = 8
+ROW = H * D
+UNIT = 4 * D
+BANK = 512
+
 FLOPS = 2 * B * H * T * S * D
 BYTES = 2 * (B * T * H * D + B * H * S * D) + 4 * B * H * T * S
 
-PIN = False
 BIG_BUFS = 9
-LAG_M = 3
-QUOTA = 3
-T_COPY = 440
-T_QUANT = 465
+LAG = 3
+RUN = 3
 
 
 def tile_attentionweightedvalues_kernel(
@@ -30,38 +30,40 @@ def tile_attentionweightedvalues_kernel(
 ):
     nc = tc.nc
     g_view = grad_out.rearrange("b (p j) c -> b p (j c)", j=J)
-    v_view = v.rearrange("b h (p i) d -> b p h (i d)", i=4)
+    v_view = v.rearrange("b h (p i) d -> b p h (i d)", i=S // P)
     o_view = out.rearrange("b h (p j) s -> b h p (j s)", j=J)
 
     with ExitStack() as ctx:
         const = ctx.enter_context(tc.tile_pool(name="const", bufs=1))
         big = ctx.enter_context(tc.tile_pool(name="big", bufs=BIG_BUFS))
-        grp = ctx.enter_context(tc.tile_pool(name="grp", bufs=3))
-        cod = ctx.enter_context(tc.tile_pool(name="cod", bufs=1))
-        tp = ctx.enter_context(tc.psum_pool(name="tp", bufs=4))
-        accp = ctx.enter_context(tc.psum_pool(name="accp", bufs=4))
-        if PIN:
-            ctx.enter_context(tc.manual_schedule())
+        grouped_pool = ctx.enter_context(tc.tile_pool(name="grouped", bufs=3))
+        mx_pool = ctx.enter_context(tc.tile_pool(name="mx", bufs=1))
+        turned_pool = ctx.enter_context(tc.psum_pool(name="turned", bufs=4))
+        sums_pool = ctx.enter_context(tc.psum_pool(name="sums", bufs=4))
+        ctx.enter_context(tc.manual_schedule())
 
-        ident = const.tile([P, P], F32, name="ident")
-        make_identity(nc, ident[:])
+        identity = const.tile([P, P], F32, name="identity")
+        make_identity(nc, identity[:])
 
-        v_raw = [big.tile([P, H, 4 * D], BF16, tag="big", name="v_raw%d" % b) for b in range(B)]
+        v_raw = [big.tile([P, H, UNIT], BF16, tag="big", name="v_raw%d" % b) for b in range(B)]
         g_raw = [
-            [big.tile([P, 4 * H * D], BF16, tag="big", name="g_raw%d_%d" % (b, q)) for q in range(2)]
+            [big.tile([P, 4 * ROW], BF16, tag="big", name="g_raw%d_%d" % (b, n)) for n in range(2)]
             for b in range(B)
         ]
-        w = 4 * H * D
-        nc.sync.dma_start(out=v_raw[0][:, 0, :], in_=v_view[0, :, 0, :])
-        nc.sync.dma_start(out=v_raw[0][:, 1, :], in_=v_view[0, :, 1, :])
-        nc.sync.dma_start(out=g_raw[0][0][:, 0 : w // 2], in_=g_view[0, :, 0 : w // 2])
-        nc.sync.dma_start(out=g_raw[0][0][:, w // 2 : w], in_=g_view[0, :, w // 2 : w])
-        nc.sync.dma_start(out=g_raw[0][1][:], in_=g_view[0, :, w : 2 * w])
-        nc.sync.dma_start(out=v_raw[0][:, 2:4, :], in_=v_view[0, :, 2:4, :])
-        nc.sync.dma_start(out=v_raw[1][:, 0, :], in_=v_view[1, :, 0, :])
-        nc.sync.dma_start(out=g_raw[1][0][:], in_=g_view[1, :, 0:w])
-        nc.sync.dma_start(out=g_raw[1][1][:], in_=g_view[1, :, w : 2 * w])
-        nc.sync.dma_start(out=v_raw[1][:, 1:4, :], in_=v_view[1, :, 1:4, :])
+        loads = [
+            (v_raw[0][:, 0, :], v_view[0, :, 0, :]),
+            (v_raw[0][:, 1, :], v_view[0, :, 1, :]),
+            (g_raw[0][0][:, 0 : 2 * ROW], g_view[0, :, 0 : 2 * ROW]),
+            (g_raw[0][0][:, 2 * ROW : 4 * ROW], g_view[0, :, 2 * ROW : 4 * ROW]),
+            (g_raw[0][1][:], g_view[0, :, 4 * ROW : 8 * ROW]),
+            (v_raw[0][:, 2:4, :], v_view[0, :, 2:4, :]),
+            (v_raw[1][:, 0, :], v_view[1, :, 0, :]),
+            (g_raw[1][0][:], g_view[1, :, 0 : 4 * ROW]),
+            (g_raw[1][1][:], g_view[1, :, 4 * ROW : 8 * ROW]),
+            (v_raw[1][:, 1:4, :], v_view[1, :, 1:4, :]),
+        ]
+        for dst, src in loads:
+            nc.sync.dma_start(out=dst, in_=src)
 
         units = [("V", 0, 0), ("V", 0, 1)] + [("G", 0, j) for j in range(J)]
         units += [("V", 0, 2), ("V", 0, 3), ("V", 1, 0)] + [("G", 1, j) for j in range(J)]
@@ -70,128 +72,132 @@ def tile_attentionweightedvalues_kernel(
         for k, unit in enumerate(units):
             place[unit] = k
 
-        todo = []
+        passes = []
         for j in range(J):
-            todo += [(0, 0, j), (0, 1, j)]
+            passes += [(0, 0, j), (0, 1, j)]
         for b, h in ((0, 2), (0, 3), (1, 0), (1, 1), (1, 2), (1, 3)):
-            todo += [(b, h, j) for j in range(J)]
+            passes += [(b, h, j) for j in range(J)]
 
-        banks = {}
+        turned = {}
         grouped = {}
-        codes = {}
-        accs = {}
-        outs = {}
+        mx = {}
+        sums = {}
+        results = {}
 
-        def transposes(unit):
+        def transpose_unit(unit):
             kind, b, x = unit
             if kind == "V":
-                src = v_raw[b][:, x, :].bitcast(F32)
+                words = v_raw[b][:, x, :].bitcast(F32)
             else:
-                src = g_raw[b][x // 4][:, (x % 4) * 2048 : (x % 4 + 1) * 2048].bitcast(F32)
-            lst = []
+                words = g_raw[b][x // 4][:, (x % 4) * UNIT : (x % 4 + 1) * UNIT].bitcast(F32)
+            turned[unit] = []
             for n in range(2):
-                bank = tp.tile([P, 4, P], F32, tag="tp", name="tpb")
-                for s in range(4):
-                    o = (4 * n + s) * P
-                    nc.tensor.transpose(out=bank[:, s, :], in_=src[:, o : o + P], identity=ident[:])
-                lst.append(bank)
-            banks[unit] = lst
+                bank = turned_pool.tile([P, 4, P], F32, tag="turned", name="turned")
+                for c in range(4):
+                    first = (4 * n + c) * P
+                    nc.tensor.transpose(
+                        out=bank[:, c, :], in_=words[:, first : first + P], identity=identity[:]
+                    )
+                turned[unit].append(bank)
 
-        def copy_out(unit, n):
-            kind = unit[0]
+        def copy_bank(unit, n):
             if unit not in grouped:
-                grouped[unit] = grp.tile([P, 2048], BF16, tag="grp", name="grp", align_bytes=64)
-            gf = grouped[unit][:].bitcast(F32)
-            bank = banks[unit][n]
-            if kind == "V":
-                dst = gf.rearrange("p (r a x) -> p a r x", a=2, x=4)[:, n]
+                grouped[unit] = grouped_pool.tile(
+                    [P, UNIT], BF16, tag="grouped", name="grouped", align_bytes=64
+                )
+            words = grouped[unit][:].bitcast(F32)
+            bank = turned[unit][n]
+            if unit[0] == "V":
+                dst = words.rearrange("p (r n x) -> p n r x", n=2, x=4)[:, n]
                 src = bank[:].rearrange("p x r -> p r x")
                 nc.scalar.copy(out=dst, in_=src)
             else:
-                dst = gf[:, n * 512 : (n + 1) * 512].rearrange("p (x r u) -> p x r u", x=2, u=2)
-                src = bank[:].rearrange("p (x u) r -> p x r u", u=2)
+                dst = words[:, n * BANK : (n + 1) * BANK].rearrange(
+                    "p (h r u) -> p h r u", h=2, u=2
+                )
+                src = bank[:].rearrange("p (h u) r -> p h r u", u=2)
                 if n == 0:
                     nc.vector.tensor_copy(out=dst, in_=src)
                 else:
                     nc.scalar.copy(out=dst, in_=src)
 
-        def quantise(unit):
-            c = cod.tile([P, 512], U32, name="c%s%d_%d" % unit, align_bytes=64)
-            s = cod.tile([P, 512], U8, name="s%s%d_%d" % unit, align_bytes=64)
-            fmt = E4 if unit[0] == "V" else E5
-            nc.vector.quantize_mx(out=c[:].bitcast(fmt), scales=s[:], in_=grouped[unit][:])
-            codes[unit] = (c, s)
+        def quantise_unit(unit):
+            words = mx_pool.tile([P, UNIT // 4], U32, name="words_%s%d_%d" % unit, align_bytes=64)
+            scales = mx_pool.tile([P, UNIT // 4], U8, name="scales_%s%d_%d" % unit, align_bytes=64)
+            fmt = E4M3_X4 if unit[0] == "V" else E5M2_X4
+            nc.vector.quantize_mx(out=words[:].bitcast(fmt), scales=scales[:], in_=grouped[unit][:])
+            mx[unit] = (words, scales)
 
         def multiply(b, h, j):
-            gc, gs = codes[("G", b, j)]
-            vc, vs = codes[("V", b, h)]
-            acc = accp.tile([P, S], F32, tag="acc", name="acc")
+            g_words, g_scales = mx[("G", b, j)]
+            v_words, v_scales = mx[("V", b, h)]
+            bank = sums_pool.tile([P, BANK], F32, tag="sums", name="sums")
             nc.tensor.matmul_mx(
-                out=acc[:],
-                lhsT=gc[:, h * P : (h + 1) * P].bitcast(E5),
-                lhsT_scale=gs[:, h * P : (h + 1) * P],
-                rhs=vc[:].bitcast(E4),
-                rhs_scale=vs[:],
+                out=bank[:],
+                lhsT=g_words[:, h * P : (h + 1) * P].bitcast(E5M2_X4),
+                lhsT_scale=g_scales[:, h * P : (h + 1) * P],
+                rhs=v_words[:].bitcast(E4M3_X4),
+                rhs_scale=v_scales[:],
                 start=True,
                 stop=True,
             )
-            accs[(b, h, j)] = acc
+            sums[(b, h, j)] = bank
 
-        def empty(b, h, j, on_vector):
-            key = (b, h)
-            if key not in outs:
-                outs[key] = big.tile([P, J * S], F32, tag="big", name="ot%d_%d" % key)
-            ot = outs[key]
-            dst = ot[:, j * S : (j + 1) * S]
+        def empty_bank(b, h, j, on_vector):
+            if (b, h) not in results:
+                results[(b, h)] = big.tile([P, J * S], F32, tag="big", name="result%d_%d" % (b, h))
+            dst = results[(b, h)][:, j * S : (j + 1) * S]
             if on_vector:
-                nc.vector.tensor_copy(out=dst, in_=accs[(b, h, j)][:])
+                nc.vector.tensor_copy(out=dst, in_=sums[(b, h, j)][:])
             else:
-                nc.scalar.copy(out=dst, in_=accs[(b, h, j)][:])
+                nc.scalar.copy(out=dst, in_=sums[(b, h, j)][:])
             if j == J - 1:
-                nc.sync.dma_start(out=o_view[b, h], in_=ot[:])
+                nc.sync.dma_start(out=o_view[b, h], in_=results[(b, h)][:])
 
-        n_units = len(units)
-        work_v = 0
-        work_s = 0
-        done = 0
+        given_vector = 0
+        given_scalar = 0
+        issued = 0
         s = 0
-        while s < n_units + 2 or done < len(todo):
-            a = units[s - 1] if 1 <= s <= n_units else None
-            q = units[s - 2] if 2 <= s <= n_units + 1 else None
+        while s < len(units) + 2 or issued < len(passes):
+            copied = units[s - 1] if 1 <= s <= len(units) else None
+            quantised = units[s - 2] if 2 <= s <= len(units) + 1 else None
+
             run = []
-            while len(run) < QUOTA and done < len(todo):
-                b, h, j = todo[done]
-                if max(place[("G", b, j)], place[("V", b, h)]) > s - LAG_M:
+            while len(run) < RUN and issued < len(passes):
+                b, h, j = passes[issued]
+                if max(place[("G", b, j)], place[("V", b, h)]) > s - LAG:
                     break
-                run.append(todo[done])
-                done += 1
+                run.append(passes[issued])
+                issued += 1
             for b, h, j in run:
                 multiply(b, h, j)
-            if s < n_units:
-                transposes(units[s])
-            if q is not None:
-                work_v += T_QUANT
-            if a is not None:
-                if a[0] == "V":
-                    work_s += 2 * T_COPY
+            if s < len(units):
+                transpose_unit(units[s])
+
+            if quantised is not None:
+                given_vector += 1
+            if copied is not None:
+                given_scalar += 1
+                if copied[0] == "V":
+                    given_scalar += 1
                 else:
-                    work_v += T_COPY
-                    work_s += T_COPY
+                    given_vector += 1
             share = 0
             for k in range(len(run)):
-                if work_v <= work_s:
-                    work_v += T_COPY
+                if given_vector <= given_scalar:
+                    given_vector += 1
                     share += 1
                 else:
-                    work_s += T_COPY
-            if q is not None:
-                quantise(q)
-            if a is not None:
-                copy_out(a, 0)
+                    given_scalar += 1
+
+            if quantised is not None:
+                quantise_unit(quantised)
+            if copied is not None:
+                copy_bank(copied, 0)
             for b, h, j in run[:share]:
-                empty(b, h, j, True)
-            if a is not None:
-                copy_out(a, 1)
+                empty_bank(b, h, j, True)
+            if copied is not None:
+                copy_bank(copied, 1)
             for b, h, j in run[share:]:
-                empty(b, h, j, False)
+                empty_bank(b, h, j, False)
             s += 1

from contextlib import ExitStack

import concourse.mybir as mybir
from concourse.masks import make_identity

BF16 = mybir.dt.bfloat16
F32 = mybir.dt.float32
U32 = mybir.dt.uint32
U8 = mybir.dt.uint8
E4M3_X4 = mybir.dt.float8_e4m3fn_x4
E5M2_X4 = mybir.dt.float8_e5m2_x4

P = 128
B, H, T, S, D = 2, 4, 1024, 512, 512
J = T // P
ROW = H * D
UNIT = 4 * D
BANK = 512

FLOPS = 2 * B * H * T * S * D
BYTES = 2 * (B * T * H * D + B * H * S * D) + 4 * B * H * T * S

BIG_BUFS = 9
LAG = 3
RUN = 3


def tile_attentionweightedvalues_kernel(
    tc, attn_weights, v, batch_size, tgt_len, grad_out, out
):
    nc = tc.nc
    g_view = grad_out.rearrange("b (p j) c -> b p (j c)", j=J)
    v_view = v.rearrange("b h (p i) d -> b p h (i d)", i=S // P)
    o_view = out.rearrange("b h (p j) s -> b h p (j s)", j=J)

    with ExitStack() as ctx:
        const = ctx.enter_context(tc.tile_pool(name="const", bufs=1))
        big = ctx.enter_context(tc.tile_pool(name="big", bufs=BIG_BUFS))
        grouped_pool = ctx.enter_context(tc.tile_pool(name="grouped", bufs=3))
        mx_pool = ctx.enter_context(tc.tile_pool(name="mx", bufs=1))
        turned_pool = ctx.enter_context(tc.psum_pool(name="turned", bufs=4))
        sums_pool = ctx.enter_context(tc.psum_pool(name="sums", bufs=4))
        ctx.enter_context(tc.manual_schedule())

        identity = const.tile([P, P], F32, name="identity")
        make_identity(nc, identity[:])

        v_raw = [big.tile([P, H, UNIT], BF16, tag="big", name="v_raw%d" % b) for b in range(B)]
        g_raw = [
            [big.tile([P, 4 * ROW], BF16, tag="big", name="g_raw%d_%d" % (b, n)) for n in range(2)]
            for b in range(B)
        ]
        loads = [
            (v_raw[0][:, 0, :], v_view[0, :, 0, :]),
            (v_raw[0][:, 1, :], v_view[0, :, 1, :]),
            (g_raw[0][0][:, 0 : 2 * ROW], g_view[0, :, 0 : 2 * ROW]),
            (g_raw[0][0][:, 2 * ROW : 4 * ROW], g_view[0, :, 2 * ROW : 4 * ROW]),
            (g_raw[0][1][:], g_view[0, :, 4 * ROW : 8 * ROW]),
            (v_raw[0][:, 2:4, :], v_view[0, :, 2:4, :]),
            (v_raw[1][:, 0, :], v_view[1, :, 0, :]),
            (g_raw[1][0][:], g_view[1, :, 0 : 4 * ROW]),
            (g_raw[1][1][:], g_view[1, :, 4 * ROW : 8 * ROW]),
            (v_raw[1][:, 1:4, :], v_view[1, :, 1:4, :]),
        ]
        for dst, src in loads:
            nc.sync.dma_start(out=dst, in_=src)

        units = [("V", 0, 0), ("V", 0, 1)] + [("G", 0, j) for j in range(J)]
        units += [("V", 0, 2), ("V", 0, 3), ("V", 1, 0)] + [("G", 1, j) for j in range(J)]
        units += [("V", 1, 1), ("V", 1, 2), ("V", 1, 3)]
        place = {}
        for k, unit in enumerate(units):
            place[unit] = k

        passes = []
        for j in range(J):
            passes += [(0, 0, j), (0, 1, j)]
        for b, h in ((0, 2), (0, 3), (1, 0), (1, 1), (1, 2), (1, 3)):
            passes += [(b, h, j) for j in range(J)]

        turned = {}
        grouped = {}
        mx = {}
        sums = {}
        results = {}

        def transpose_unit(unit):
            kind, b, x = unit
            if kind == "V":
                words = v_raw[b][:, x, :].bitcast(F32)
            else:
                words = g_raw[b][x // 4][:, (x % 4) * UNIT : (x % 4 + 1) * UNIT].bitcast(F32)
            turned[unit] = []
            for n in range(2):
                bank = turned_pool.tile([P, 4, P], F32, tag="turned", name="turned")
                for c in range(4):
                    first = (4 * n + c) * P
                    nc.tensor.transpose(
                        out=bank[:, c, :], in_=words[:, first : first + P], identity=identity[:]
                    )
                turned[unit].append(bank)

        def copy_bank(unit, n):
            if unit not in grouped:
                grouped[unit] = grouped_pool.tile(
                    [P, UNIT], BF16, tag="grouped", name="grouped", align_bytes=64
                )
            words = grouped[unit][:].bitcast(F32)
            bank = turned[unit][n]
            if unit[0] == "V":
                dst = words.rearrange("p (r n x) -> p n r x", n=2, x=4)[:, n]
                src = bank[:].rearrange("p x r -> p r x")
                nc.scalar.copy(out=dst, in_=src)
            else:
                dst = words[:, n * BANK : (n + 1) * BANK].rearrange(
                    "p (h r u) -> p h r u", h=2, u=2
                )
                src = bank[:].rearrange("p (h u) r -> p h r u", u=2)
                if n == 0:
                    nc.vector.tensor_copy(out=dst, in_=src)
                else:
                    nc.scalar.copy(out=dst, in_=src)

        def quantise_unit(unit):
            words = mx_pool.tile([P, UNIT // 4], U32, name="words_%s%d_%d" % unit, align_bytes=64)
            scales = mx_pool.tile([P, UNIT // 4], U8, name="scales_%s%d_%d" % unit, align_bytes=64)
            fmt = E4M3_X4 if unit[0] == "V" else E5M2_X4
            nc.vector.quantize_mx(out=words[:].bitcast(fmt), scales=scales[:], in_=grouped[unit][:])
            mx[unit] = (words, scales)

        def multiply(b, h, j):
            g_words, g_scales = mx[("G", b, j)]
            v_words, v_scales = mx[("V", b, h)]
            bank = sums_pool.tile([P, BANK], F32, tag="sums", name="sums")
            nc.tensor.matmul_mx(
                out=bank[:],
                lhsT=g_words[:, h * P : (h + 1) * P].bitcast(E5M2_X4),
                lhsT_scale=g_scales[:, h * P : (h + 1) * P],
                rhs=v_words[:].bitcast(E4M3_X4),
                rhs_scale=v_scales[:],
                start=True,
                stop=True,
            )
            sums[(b, h, j)] = bank

        def empty_bank(b, h, j, on_vector):
            if (b, h) not in results:
                results[(b, h)] = big.tile([P, J * S], F32, tag="big", name="result%d_%d" % (b, h))
            dst = results[(b, h)][:, j * S : (j + 1) * S]
            if on_vector:
                nc.vector.tensor_copy(out=dst, in_=sums[(b, h, j)][:])
            else:
                nc.scalar.copy(out=dst, in_=sums[(b, h, j)][:])
            if j == J - 1:
                nc.sync.dma_start(out=o_view[b, h], in_=results[(b, h)][:])

        given_vector = 0
        given_scalar = 0
        issued = 0
        s = 0
        while s < len(units) + 2 or issued < len(passes):
            copied = units[s - 1] if 1 <= s <= len(units) else None
            quantised = units[s - 2] if 2 <= s <= len(units) + 1 else None

            run = []
            while len(run) < RUN and issued < len(passes):
                b, h, j = passes[issued]
                if max(place[("G", b, j)], place[("V", b, h)]) > s - LAG:
                    break
                run.append(passes[issued])
                issued += 1
            for b, h, j in run:
                multiply(b, h, j)
            if s < len(units):
                transpose_unit(units[s])

            if quantised is not None:
                given_vector += 1
            if copied is not None:
                given_scalar += 1
                if copied[0] == "V":
                    given_scalar += 1
                else:
                    given_vector += 1
            share = 0
            for k in range(len(run)):
                if given_vector <= given_scalar:
                    given_vector += 1
                    share += 1
                else:
                    given_scalar += 1

            if quantised is not None:
                quantise_unit(quantised)
            if copied is not None:
                copy_bank(copied, 0)
            for b, h, j in run[:share]:
                empty_bank(b, h, j, True)
            if copied is not None:
                copy_bank(copied, 1)
            for b, h, j in run[share:]:
                empty_bank(b, h, j, False)
            s += 1
